import numpy as np
import ml_dtypes


def mxq(x, axis, fmt="e4m3"):
    dtype, down = {"e4m3": (ml_dtypes.float8_e4m3fn, 7), "e5m2": (ml_dtypes.float8_e5m2, 14)}[fmt]
    v = np.moveaxis(np.asarray(x, np.float32).astype(ml_dtypes.bfloat16).astype(np.float64), axis, -1)
    blocks = v.reshape(v.shape[:-1] + (-1, 32))
    amax = np.abs(blocks).max(-1, keepdims=True)
    byte = np.maximum(np.where(amax > 0, np.frexp(amax)[1] - 1 + 127, 0) - down, 1)
    scale = np.exp2(byte - 127.0)
    codes = (blocks / scale).astype(np.float32).astype(dtype).astype(np.float64)
    return np.moveaxis((codes * scale).reshape(v.shape), -1, axis)


WIDE = False


def mx_kscale(k):
    if not WIDE:
        return np.ones(k)
    levels = np.array([18, -18])
    if k % 512:
        return np.exp2(np.random.permutation(np.resize(levels, k // 32))).repeat(32)
    a = np.empty((k // 512, 16))
    for p in range(k // 512):
        a[p, :8] = np.random.permutation(np.resize(levels, 8))
        for g in range(8):
            far = levels[np.abs(levels - a[p, g]) >= 10]
            a[p, g + 8] = far[np.random.randint(len(far))]
    return np.exp2(a.ravel()).repeat(32)


BF16 = ml_dtypes.bfloat16


def bf(x):
    return np.asarray(x, np.float32).astype(BF16)


def f64(x):
    return np.asarray(x).astype(np.float64)


S, B, D1, D2 = 8, 512, 512, 512


def sample(eps, logvar, mean):
    return eps * np.exp(0.5 * logvar) + mean


def setup_inputs():
    s = mx_kscale(S * B).reshape(S, B, 1)
    u = mx_kscale(D2)
    h00 = bf(np.maximum(np.random.standard_normal((S, B, D1)), 0.0) * 1.1)
    wm10 = bf(np.random.standard_normal((D1, D2)) * 0.8 / np.sqrt(D1))
    wv1 = bf(2.0 * np.log(0.6 / np.sqrt(D1)) + 0.5 * np.random.standard_normal((D1, D2)))
    bm1 = bf(np.random.standard_normal(D2) * 0.3)
    bv1 = bf(2.0 * np.log(0.3) + 0.5 * np.random.standard_normal(D2))
    we10 = bf(np.random.standard_normal((S, D1, D2)))
    be1 = bf(np.random.standard_normal((S, 1, D2)))
    g = bf(np.random.standard_normal((S, B, D2)) * np.exp2(np.random.randint(-6, 1, (S, B, 1))) / s * u)
    z = f64(h00) @ sample(f64(we10), f64(wv1), f64(wm10)) + sample(f64(be1), f64(bv1), f64(bm1))
    return {
        "h0": bf(f64(h00) * s),
        "wm1": bf(f64(wm10) / u),
        "wv1": wv1,
        "bm1": bm1,
        "bv1": bv1,
        "we1": bf(f64(we10) / u),
        "be1": be1,
        "z": np.asarray(z, np.float32),
        "grad_out": g,
    }


def reference(h0, wm1, wv1, bm1, bv1, we1, be1, z, grad_out):
    dz = np.where(f64(z) > 0.0, f64(grad_out), 0.0)
    w1 = sample(f64(we1), f64(wv1), f64(wm1))
    dh0 = mxq(dz, 2, "e5m2") @ mxq(w1, 2, "e4m3").transpose(0, 2, 1)
    ht = f64(h0).reshape(S * B, D1)
    dzt = dz.reshape(S * B, D2)
    dwm1 = mxq(ht, 0, "e4m3").T @ mxq(dzt, 0, "e5m2")
    return dh0, dwm1

@@ -1,0 +1,216 @@
+from contextlib import ExitStack
+
+import concourse.mybir as mybir
+from concourse.masks import make_identity
+
+S, B, D1, D2 = 8, 512, 512, 512
+FLOPS = 2 * 2 * S * B * D1 * D2
+BYTES = S * B * (2 * D1 + 4 * D2 + 2 * D2 + 4 * D1) + 2 * S * D1 * D2 + (2 + 2 + 4) * D1 * D2
+
+F32 = mybir.dt.float32
+BF16 = mybir.dt.bfloat16
+U32 = mybir.dt.uint32
+U8 = mybir.dt.uint8
+E4M3 = mybir.dt.float8_e4m3fn_x4
+E5M2 = mybir.dt.float8_e5m2_x4
+ALU = mybir.AluOpType
+ACT = mybir.ActivationFunctionType
+
+P = 128
+H_SPLIT = 128
+
+
+def tile_bnn_pb_v_kernel(tc, h0, wm1, wv1, bm1, bv1, we1, be1, z, grad_out, out_0, out_1):
+    nc = tc.nc
+    with ExitStack() as ctx:
+        const = ctx.enter_context(tc.tile_pool(name="const", bufs=1))
+        loads = ctx.enter_context(tc.tile_pool(name="loads", bufs=4))
+        mid = ctx.enter_context(tc.tile_pool(name="mid", bufs=2))
+        codes = ctx.enter_context(tc.tile_pool(name="codes", bufs=2))
+        outs = ctx.enter_context(tc.tile_pool(name="outs", bufs=3))
+        acc_pool = ctx.enter_context(tc.psum_pool(name="acc", bufs=1))
+        psum = ctx.enter_context(tc.psum_pool(name="psum", bufs=4))
+
+        ident_f = const.tile([P, P], F32, name="ident_f")
+        make_identity(nc, ident_f[:])
+        ident_b = const.tile([P, P], BF16, name="ident_b")
+        make_identity(nc, ident_b[:])
+
+        acc = [acc_pool.tile([P, D2], F32, name="acc%d" % b) for b in range(4)]
+
+        we_t, z_t, g_t, h_t = {}, {}, {}, {}
+        hi_t, p_t, wt_t, dz_t, dt_t = {}, {}, {}, {}, {}
+        wq_t, dq_t, hq_t, tq_t, o_t = {}, {}, {}, {}, {}
+
+        def load_we(s):
+            we_t[s] = loads.tile([P, 4, D2], BF16, name="we")
+            nc.sync.dma_start(out=we_t[s][:], in_=we1[s].rearrange("(p j) w -> p j w", j=4))
+
+        def load_zg(s):
+            z_t[s] = loads.tile([P, 4, D2], F32, name="z")
+            nc.sync.dma_start(out=z_t[s][:], in_=z[s].rearrange("(p j) w -> p j w", j=4))
+            g_t[s] = loads.tile([P, 4, D2], BF16, name="g")
+            nc.sync.dma_start(out=g_t[s][:], in_=grad_out[s].rearrange("(p j) w -> p j w", j=4))
+
+        def load_h(s):
+            h_t[s] = loads.tile([P, 4, D1], BF16, name="h")
+            nc.sync.dma_start(out=h_t[s][:], in_=h0[s].rearrange("(p j) w -> p j w", j=4))
+
+        def quantize(s, src, dtype, store, nm):
+            c = codes.tile([P, 512], U32, name=nm + "c", align_bytes=256)
+            q = codes.tile([P, 512], U8, name=nm + "s", align_bytes=256)
+            nc.vector.quantize_mx(out=c[:].bitcast(dtype), scales=q[:], in_=src)
+            store[s] = (c, q)
+
+        def mask(s):
+            dz_t[s] = mid.tile([P, D2, 4], BF16, name="dz", align_bytes=256)
+            nc.vector.scalar_tensor_tensor(
+                out=dz_t[s][:],
+                in0=z_t[s][:].rearrange("p j w -> p w j"),
+                scalar=0.0,
+                in1=g_t[s][:].rearrange("p j w -> p w j"),
+                op0=ALU.is_gt,
+                op1=ALU.mult,
+            )
+
+        def h_part(s, lo, hi, copy):
+            copy(
+                out=hi_t[s][:, lo:hi, :].rearrange("p (c i) t -> p c t i", i=4),
+                in_=h_t[s][:, :, lo:hi].rearrange("p t (c i) -> p c t i", i=4),
+            )
+
+        def h_vector(s):
+            h_part(s, 0, H_SPLIT, nc.vector.tensor_copy)
+
+        def h_scalar(s):
+            hi_t[s] = mid.tile([P, D1, 4], BF16, name="hi", align_bytes=256)
+            h_part(s, H_SPLIT, D1, nc.scalar.copy)
+
+        def product(s, js):
+            nc.vector.tensor_tensor(
+                out=p_t[s][:, js, :, :],
+                in0=we_t[s][:, js, :].rearrange("p j (m t) -> p j t m", t=4),
+                in1=e_s[:, js, :, :],
+                op=ALU.mult,
+            )
+
+        def weight_transposes(s):
+            wt_t[s] = mid.tile([P, 4, P, 4], BF16, name="wt", align_bytes=256)
+            for j in range(4):
+                bank = psum.tile([P, 4, P], F32, name="bank")
+                for t in range(4):
+                    nc.tensor.matmul(bank[:, t, :], lhsT=wm_s[:, j, t, :], rhs=ident_f[:], is_transpose=True, start=True, stop=False)
+                    nc.tensor.matmul(bank[:, t, :], lhsT=p_t[s][:, j, t, :], rhs=ident_f[:], is_transpose=True, start=False, stop=True)
+                nc.scalar.copy(out=wt_t[s][:, j, :, :], in_=bank[:].rearrange("p t x -> p x t"))
+
+        def dz_transposes(s):
+            dt_t[s] = mid.tile([P, 4, P, 4], BF16, name="dt", align_bytes=256)
+            view = dz_t[s][:].rearrange("p (m t) j -> p m t j", t=4)
+            for jj in range(2):
+                bank = psum.tile([P, 2, 4, P], BF16, name="bank")
+                for j in range(2):
+                    for t in range(4):
+                        nc.tensor.transpose(bank[:, j, t, :], view[:, :, t, 2 * jj + j], ident_b[:])
+                nc.scalar.copy(out=dt_t[s][:, 2 * jj : 2 * jj + 2, :, :], in_=bank[:].rearrange("p j t x -> p j x t"))
+
+        def weight_grad(s):
+            hc, hs = hq_t[s]
+            dc, ds = dq_t[s]
+            for b in range(4):
+                cols = slice(P * b, P * (b + 1))
+                nc.tensor.matmul_mx(
+                    out=acc[b][:],
+                    lhsT=hc[:, cols].bitcast(E4M3),
+                    lhsT_scale=hs[:, cols],
+                    rhs=dc[:].bitcast(E5M2),
+                    rhs_scale=ds[:],
+                    start=(s == 0),
+                    stop=(s == S - 1),
+                )
+
+        def input_grad(s):
+            tcod, tsc = tq_t[s]
+            wc, ws = wq_t[s]
+            o_t[s] = outs.tile([P, 4, P, 4], F32, name="o")
+            for j in range(4):
+                cols = slice(P * j, P * (j + 1))
+                bank = psum.tile([P, 4, P], F32, name="bank")
+                nc.tensor.matmul_mx(
+                    out=bank[:].rearrange("p t x -> p (t x)"),
+                    lhsT=tcod[:, cols].bitcast(E5M2),
+                    lhsT_scale=tsc[:, cols],
+                    rhs=wc[:].bitcast(E4M3),
+                    rhs_scale=ws[:],
+                    start=True,
+                    stop=True,
+                )
+                nc.scalar.copy(out=o_t[s][:, j, :, :], in_=bank[:].rearrange("p t x -> p x t"))
+
+        def store(s):
+            nc.sync.dma_start(
+                out=out_0[s].rearrange("(p j) d -> p j d", j=4),
+                in_=o_t[s][:].rearrange("p j x t -> p j (x t)"),
+            )
+
+        with tc.manual_schedule():
+            warm = const.tile([P, 1], F32, name="warm")
+            nc.vector.memset(warm[:], 0.0)
+            nc.scalar.activation(out=warm[:], in_=warm[:], func=ACT.Exp)
+            wv_t = const.tile([P, 4, D2], BF16, name="wv_t")
+            wv_view = wv1.rearrange("(p j) w -> p j w", j=4)
+            nc.sync.dma_start(out=wv_t[:], in_=wv_view)
+            load_we(0)
+            load_zg(0)
+            wm_t = const.tile([P, 4, D2], BF16, name="wm_t")
+            nc.sync.dma_start(out=wm_t[:], in_=wm1.rearrange("(p j) w -> p j w", j=4))
+            load_h(0)
+            for s in (1, 2):
+                load_we(s)
+                load_zg(s)
+                load_h(s)
+
+            e_s = const.tile([P, 4, 4, P], F32, name="e_s")
+            wm_s = const.tile([P, 4, 4, P], F32, name="wm_s")
+            for j in range(4):
+                nc.scalar.activation(
+                    out=e_s[:, j, :, :],
+                    in_=wv_t[:, j, :].rearrange("p (m t) -> p t m", t=4),
+                    func=ACT.Exp,
+                    scale=0.5,
+                )
+            p_t[0] = mid.tile([P, 4, 4, P], F32, name="p")
+            for j in range(4):
+                product(0, slice(j, j + 1))
+            nc.scalar.copy(out=wm_s[:], in_=wm_t[:].rearrange("p j (m t) -> p j t m", t=4))
+            h_scalar(0)
+            weight_transposes(0)
+
+            for s in range(S):
+                if s + 3 < S:
+                    load_we(s + 3)
+                    load_zg(s + 3)
+                    load_h(s + 3)
+                mask(s)
+                if s == 0:
+                    h_vector(0)
+                if s + 1 < S:
+                    h_scalar(s + 1)
+                dz_transposes(s)
+                quantize(s, hi_t[s][:].rearrange("p w j -> p (w j)"), E4M3, hq_t, "h")
+                quantize(s, dz_t[s][:].rearrange("p w j -> p (w j)"), E5M2, dq_t, "d")
+                weight_grad(s)
+                quantize(s, wt_t[s][:].rearrange("p j x t -> p (j x t)"), E4M3, wq_t, "w")
+                if s + 1 < S:
+                    h_vector(s + 1)
+                quantize(s, dt_t[s][:].rearrange("p j x t -> p (j x t)"), E5M2, tq_t, "t")
+                input_grad(s)
+                store(s)
+                if s + 1 < S:
+                    p_t[s + 1] = mid.tile([P, 4, 4, P], F32, name="p")
+                    product(s + 1, slice(0, 4))
+                    weight_transposes(s + 1)
+
+            for b in range(4):
+                r = outs.tile([P, D2], F32, name="r")
+                nc.vector.tensor_copy(out=r[:], in_=acc[b][:])
+                nc.sync.dma_start(out=out_1[P * b : P * (b + 1), :], in_=r[:])

@@ -17,7 +17,6 @@ ALU = mybir.AluOpType
 ACT = mybir.ActivationFunctionType
 
 P = 128
-H_SPLIT = 128
 
 
 def tile_bnn_pb_v_kernel(tc, h0, wm1, wv1, bm1, bv1, we1, be1, z, grad_out, out_0, out_1):
@@ -33,13 +32,11 @@ def tile_bnn_pb_v_kernel(tc, h0, wm1, wv1, bm1, bv1, we1, be1, z, grad_out, out_
 
         ident_f = const.tile([P, P], F32, name="ident_f")
         make_identity(nc, ident_f[:])
-        ident_b = const.tile([P, P], BF16, name="ident_b")
-        make_identity(nc, ident_b[:])
 
         acc = [acc_pool.tile([P, D2], F32, name="acc%d" % b) for b in range(4)]
 
         we_t, z_t, g_t, h_t = {}, {}, {}, {}
-        hi_t, p_t, wt_t, dz_t, dt_t = {}, {}, {}, {}, {}
+        hi_t, di_t, p_t, wt_t, dz_t, dt_t = {}, {}, {}, {}, {}, {}
         wq_t, dq_t, hq_t, tq_t, o_t = {}, {}, {}, {}, {}
 
         def load_we(s):
@@ -62,95 +59,148 @@ def tile_bnn_pb_v_kernel(tc, h0, wm1, wv1, bm1, bv1, we1, be1, z, grad_out, out_
             nc.vector.quantize_mx(out=c[:].bitcast(dtype), scales=q[:], in_=src)
             store[s] = (c, q)
 
+        def q_h(s):
+            quantize(s, hi_t[s][:].rearrange("p w j -> p (w j)"), E4M3, hq_t, "h")
+
+        def q_d(s):
+            quantize(s, di_t[s][:].rearrange("p w j -> p (w j)"), E5M2, dq_t, "d")
+
+        def q_w(s):
+            quantize(s, wt_t[s][:].rearrange("p j x t -> p (j x t)"), E4M3, wq_t, "w")
+
+        def q_t(s):
+            quantize(s, dt_t[s][:].rearrange("p j x u -> p (j x u)").bitcast(BF16), E5M2, tq_t, "t")
+
+        def load(s):
+            load_we(s)
+            load_zg(s)
+            load_h(s)
+
         def mask(s):
-            dz_t[s] = mid.tile([P, D2, 4], BF16, name="dz", align_bytes=256)
-            nc.vector.scalar_tensor_tensor(
-                out=dz_t[s][:],
-                in0=z_t[s][:].rearrange("p j w -> p w j"),
-                scalar=0.0,
-                in1=g_t[s][:].rearrange("p j w -> p w j"),
-                op0=ALU.is_gt,
-                op1=ALU.mult,
-            )
+            dz_t[s] = mid.tile([P, 4, D2], BF16, name="dz", align_bytes=256)
+            nc.vector.scalar_tensor_tensor(out=dz_t[s][:], in0=z_t[s][:], scalar=0.0, in1=g_t[s][:], op0=ALU.is_gt, op1=ALU.mult)
 
-        def h_part(s, lo, hi, copy):
-            copy(
-                out=hi_t[s][:, lo:hi, :].rearrange("p (c i) t -> p c t i", i=4),
-                in_=h_t[s][:, :, lo:hi].rearrange("p t (c i) -> p c t i", i=4),
-            )
+        def interleave(copy, out, in_):
+            copy(out=out[:].rearrange("p (c i) t -> p c t i", i=4), in_=in_[:].rearrange("p t (c i) -> p c t i", i=4))
 
-        def h_vector(s):
-            h_part(s, 0, H_SPLIT, nc.vector.tensor_copy)
+        def d_interleave(s):
+            di_t[s] = mid.tile([P, D2, 4], BF16, name="di", align_bytes=256)
+            interleave(nc.vector.tensor_copy, di_t[s], dz_t[s])
 
-        def h_scalar(s):
+        def h_interleave(s):
             hi_t[s] = mid.tile([P, D1, 4], BF16, name="hi", align_bytes=256)
-            h_part(s, H_SPLIT, D1, nc.scalar.copy)
+            interleave(nc.scalar.copy, hi_t[s], h_t[s])
 
-        def product(s, js):
-            nc.vector.tensor_tensor(
-                out=p_t[s][:, js, :, :],
-                in0=we_t[s][:, js, :].rearrange("p j (m t) -> p j t m", t=4),
-                in1=e_s[:, js, :, :],
-                op=ALU.mult,
-            )
+        def product(s):
+            p_t[s] = mid.tile([P, 4, 4, P], F32, name="p")
+            pieces = [slice(j, j + 1) for j in range(4)] if s == 0 else [slice(0, 4)]
+            for js in pieces:
+                nc.vector.tensor_tensor(
+                    out=p_t[s][:, js, :, :],
+                    in0=we_t[s][:, js, :].rearrange("p j (m t) -> p j t m", t=4),
+                    in1=e_s[:, js, :, :],
+                    op=ALU.mult,
+                )
 
-        def weight_transposes(s):
-            wt_t[s] = mid.tile([P, 4, P, 4], BF16, name="wt", align_bytes=256)
-            for j in range(4):
-                bank = psum.tile([P, 4, P], F32, name="bank")
-                for t in range(4):
-                    nc.tensor.matmul(bank[:, t, :], lhsT=wm_s[:, j, t, :], rhs=ident_f[:], is_transpose=True, start=True, stop=False)
-                    nc.tensor.matmul(bank[:, t, :], lhsT=p_t[s][:, j, t, :], rhs=ident_f[:], is_transpose=True, start=False, stop=True)
-                nc.scalar.copy(out=wt_t[s][:, j, :, :], in_=bank[:].rearrange("p t x -> p x t"))
+        def w_transposes(s, j):
+            if j == 0:
+                wt_t[s] = mid.tile([P, 4, P, 4], BF16, name="wt", align_bytes=256)
+            bank = psum.tile([P, 4, P], F32, name="bank")
+            for t in range(4):
+                nc.tensor.matmul(bank[:, t, :], lhsT=wm_s[:, j, t, :], rhs=ident_f[:], is_transpose=True, start=True, stop=False)
+                nc.tensor.matmul(bank[:, t, :], lhsT=p_t[s][:, j, t, :], rhs=ident_f[:], is_transpose=True, start=False, stop=True)
+            nc.scalar.copy(out=wt_t[s][:, j, :, :], in_=bank[:].rearrange("p t x -> p x t"))
 
-        def dz_transposes(s):
-            dt_t[s] = mid.tile([P, 4, P, 4], BF16, name="dt", align_bytes=256)
-            view = dz_t[s][:].rearrange("p (m t) j -> p m t j", t=4)
-            for jj in range(2):
-                bank = psum.tile([P, 2, 4, P], BF16, name="bank")
-                for j in range(2):
-                    for t in range(4):
-                        nc.tensor.transpose(bank[:, j, t, :], view[:, :, t, 2 * jj + j], ident_b[:])
-                nc.scalar.copy(out=dt_t[s][:, 2 * jj : 2 * jj + 2, :, :], in_=bank[:].rearrange("p j t x -> p j x t"))
+        def dz_transposes(s, half):
+            if half == 0:
+                dt_t[s] = mid.tile([P, 4, P, 2], F32, name="dt", align_bytes=256)
+            bank = psum.tile([P, 2, 2, P], F32, name="bank")
+            for k in range(2):
+                words = dz_t[s][:, 2 * half + k, :].bitcast(F32)
+                for u in range(2):
+                    nc.tensor.transpose(bank[:, k, u, :], words[:, u::2], ident_f[:])
+            nc.scalar.copy(out=dt_t[s][:, 2 * half : 2 * half + 2, :, :], in_=bank[:].rearrange("p k u x -> p k x u"))
 
-        def weight_grad(s):
+        def weight_grad(s, b):
             hc, hs = hq_t[s]
             dc, ds = dq_t[s]
-            for b in range(4):
-                cols = slice(P * b, P * (b + 1))
-                nc.tensor.matmul_mx(
-                    out=acc[b][:],
-                    lhsT=hc[:, cols].bitcast(E4M3),
-                    lhsT_scale=hs[:, cols],
-                    rhs=dc[:].bitcast(E5M2),
-                    rhs_scale=ds[:],
-                    start=(s == 0),
-                    stop=(s == S - 1),
-                )
+            cols = slice(P * b, P * (b + 1))
+            nc.tensor.matmul_mx(
+                out=acc[b][:],
+                lhsT=hc[:, cols].bitcast(E4M3),
+                lhsT_scale=hs[:, cols],
+                rhs=dc[:].bitcast(E5M2),
+                rhs_scale=ds[:],
+                start=(s == 0),
+                stop=(s == S - 1),
+            )
+            if s == S - 1:
+                r = outs.tile([P, D2], F32, name="r%d" % b, bufs=1)
+                copy = nc.vector.tensor_copy if b < 2 else nc.scalar.copy
+                copy(out=r[:], in_=acc[b][:])
+                nc.sync.dma_start(out=out_1[P * b : P * (b + 1), :], in_=r[:])
 
-        def input_grad(s):
+        def input_grad(s, j):
             tcod, tsc = tq_t[s]
             wc, ws = wq_t[s]
-            o_t[s] = outs.tile([P, 4, P, 4], F32, name="o")
-            for j in range(4):
-                cols = slice(P * j, P * (j + 1))
-                bank = psum.tile([P, 4, P], F32, name="bank")
-                nc.tensor.matmul_mx(
-                    out=bank[:].rearrange("p t x -> p (t x)"),
-                    lhsT=tcod[:, cols].bitcast(E5M2),
-                    lhsT_scale=tsc[:, cols],
-                    rhs=wc[:].bitcast(E4M3),
-                    rhs_scale=ws[:],
-                    start=True,
-                    stop=True,
-                )
-                nc.scalar.copy(out=o_t[s][:, j, :, :], in_=bank[:].rearrange("p t x -> p x t"))
+            if j == 0:
+                o_t[s] = outs.tile([P, 4, P, 4], F32, name="o")
+            cols = slice(P * j, P * (j + 1))
+            bank = psum.tile([P, 4, P], F32, name="bank")
+            nc.tensor.matmul_mx(
+                out=bank[:].rearrange("p t x -> p (t x)"),
+                lhsT=tcod[:, cols].bitcast(E5M2),
+                lhsT_scale=tsc[:, cols],
+                rhs=wc[:].bitcast(E4M3),
+                rhs_scale=ws[:],
+                start=True,
+                stop=True,
+            )
+            on_vector = (s == S - 1 and j % 2 == 1) or (s == S - 2 and j == 3)
+            copy = nc.vector.tensor_copy if on_vector else nc.scalar.copy
+            copy(out=o_t[s][:, j, :, :], in_=bank[:].rearrange("p t x -> p x t"))
+            if s == S - 1 and j % 2 == 1:
+                store_rows(s, j - 1, j + 1)
+
+        def store_rows(s, j0, j1):
+            nc.sync.dma_start(
+                out=out_0[s].rearrange("(p j) d -> p j d", j=4)[:, j0:j1, :],
+                in_=o_t[s][:, j0:j1, :, :].rearrange("p j x t -> p j (x t)"),
+            )
 
         def store(s):
-            nc.sync.dma_start(
-                out=out_0[s].rearrange("(p j) d -> p j d", j=4),
-                in_=o_t[s][:].rearrange("p j x t -> p j (x t)"),
-            )
+            if s < S - 1:
+                store_rows(s, 0, 4)
+
+        def sub(fn, k):
+            return lambda s: fn(s, k)
+
+        STEP = [
+            (sub(weight_grad, 2), 1),
+            (sub(w_transposes, 1), 0),
+            (sub(input_grad, 0), 1),
+            (sub(weight_grad, 1), 1),
+            (product, -2),
+            (sub(weight_grad, 3), 1),
+            (sub(w_transposes, 2), 0),
+            (q_d, -1),
+            (load, -3),
+            (sub(w_transposes, 3), 0),
+            (q_w, 0),
+            (sub(input_grad, 1), 1),
+            (sub(weight_grad, 0), 1),
+            (store, 2),
+            (mask, -2),
+            (sub(input_grad, 2), 1),
+            (sub(dz_transposes, 0), -1),
+            (sub(dz_transposes, 1), -1),
+            (q_t, -1),
+            (sub(w_transposes, 0), -1),
+            (h_interleave, -2),
+            (d_interleave, -2),
+            (q_h, -1),
+            (sub(input_grad, 3), 1),
+        ]
 
         with tc.manual_schedule():
             warm = const.tile([P, 1], F32, name="warm")
@@ -158,16 +208,16 @@ def tile_bnn_pb_v_kernel(tc, h0, wm1, wv1, bm1, bv1, we1, be1, z, grad_out, out_
             nc.scalar.activation(out=warm[:], in_=warm[:], func=ACT.Exp)
             wv_t = const.tile([P, 4, D2], BF16, name="wv_t")
             wv_view = wv1.rearrange("(p j) w -> p j w", j=4)
-            nc.sync.dma_start(out=wv_t[:], in_=wv_view)
-            load_we(0)
+            we_t[0] = loads.tile([P, 4, D2], BF16, name="we")
+            we_view = we1[0].rearrange("(p j) w -> p j w", j=4)
+            for js in (slice(0, 2), slice(2, 4)):
+                nc.sync.dma_start(out=wv_t[:, js, :], in_=wv_view[:, js, :])
+                nc.sync.dma_start(out=we_t[0][:, js, :], in_=we_view[:, js, :])
             load_zg(0)
             wm_t = const.tile([P, 4, D2], BF16, name="wm_t")
             nc.sync.dma_start(out=wm_t[:], in_=wm1.rearrange("(p j) w -> p j w", j=4))
             load_h(0)
-            for s in (1, 2):
-                load_we(s)
-                load_zg(s)
-                load_h(s)
+            load(1)
 
             e_s = const.tile([P, 4, 4, P], F32, name="e_s")
             wm_s = const.tile([P, 4, 4, P], F32, name="wm_s")
@@ -178,39 +228,18 @@ def tile_bnn_pb_v_kernel(tc, h0, wm1, wv1, bm1, bv1, we1, be1, z, grad_out, out_
                     func=ACT.Exp,
                     scale=0.5,
                 )
-            p_t[0] = mid.tile([P, 4, 4, P], F32, name="p")
             for j in range(4):
-                product(0, slice(j, j + 1))
-            nc.scalar.copy(out=wm_s[:], in_=wm_t[:].rearrange("p j (m t) -> p j t m", t=4))
-            h_scalar(0)
-            weight_transposes(0)
+                nc.gpsimd.tensor_scalar(
+                    out=wm_s[:, j, :, :],
+                    in0=wm_t[:, j, :].rearrange("p (m t) -> p t m", t=4),
+                    scalar1=1.0,
+                    scalar2=0.0,
+                    op0=ALU.mult,
+                    op1=ALU.add,
+                )
 
-            for s in range(S):
-                if s + 3 < S:
-                    load_we(s + 3)
-                    load_zg(s + 3)
-                    load_h(s + 3)
-                mask(s)
-                if s == 0:
-                    h_vector(0)
-                if s + 1 < S:
-                    h_scalar(s + 1)
-                dz_transposes(s)
-                quantize(s, hi_t[s][:].rearrange("p w j -> p (w j)"), E4M3, hq_t, "h")
-                quantize(s, dz_t[s][:].rearrange("p w j -> p (w j)"), E5M2, dq_t, "d")
-                weight_grad(s)
-                quantize(s, wt_t[s][:].rearrange("p j x t -> p (j x t)"), E4M3, wq_t, "w")
-                if s + 1 < S:
-                    h_vector(s + 1)
-                quantize(s, dt_t[s][:].rearrange("p j x t -> p (j x t)"), E5M2, tq_t, "t")
-                input_grad(s)
-                store(s)
-                if s + 1 < S:
-                    p_t[s + 1] = mid.tile([P, 4, 4, P], F32, name="p")
-                    product(s + 1, slice(0, 4))
-                    weight_transposes(s + 1)
-
-            for b in range(4):
-                r = outs.tile([P, D2], F32, name="r")
-                nc.vector.tensor_copy(out=r[:], in_=acc[b][:])
-                nc.sync.dma_start(out=out_1[P * b : P * (b + 1), :], in_=r[:])
+            for step in range(-3, S + 3):
+                for what, lag in STEP:
+                    s = step - lag
+                    if 0 <= s < S and not (what is load and s < 2):
+                        what(s)

@@ -17,6 +17,7 @@ ALU = mybir.AluOpType
 ACT = mybir.ActivationFunctionType
 
 P = 128
+H_SPLIT = 128
 
 
 def tile_bnn_pb_v_kernel(tc, h0, wm1, wv1, bm1, bv1, we1, be1, z, grad_out, out_0, out_1):
@@ -71,28 +72,29 @@ def tile_bnn_pb_v_kernel(tc, h0, wm1, wv1, bm1, bv1, we1, be1, z, grad_out, out_
         def q_t(s):
             quantize(s, dt_t[s][:].rearrange("p j x u -> p (j x u)").bitcast(BF16), E5M2, tq_t, "t")
 
-        def load(s):
-            load_we(s)
-            load_zg(s)
-            load_h(s)
-
         def mask(s):
-            dz_t[s] = mid.tile([P, 4, D2], BF16, name="dz", align_bytes=256)
+            dz_t[s] = mid.tile([P, 4, D2], BF16, name="dz", align_bytes=256, bufs=3)
             nc.vector.scalar_tensor_tensor(out=dz_t[s][:], in0=z_t[s][:], scalar=0.0, in1=g_t[s][:], op0=ALU.is_gt, op1=ALU.mult)
 
-        def interleave(copy, out, in_):
-            copy(out=out[:].rearrange("p (c i) t -> p c t i", i=4), in_=in_[:].rearrange("p t (c i) -> p c t i", i=4))
+        def interleave(copy, out, in_, lo, hi):
+            copy(
+                out=out[:, lo:hi, :].rearrange("p (c i) t -> p c t i", i=4),
+                in_=in_[:, :, lo:hi].rearrange("p t (c i) -> p c t i", i=4),
+            )
 
         def d_interleave(s):
             di_t[s] = mid.tile([P, D2, 4], BF16, name="di", align_bytes=256)
-            interleave(nc.vector.tensor_copy, di_t[s], dz_t[s])
+            interleave(nc.vector.tensor_copy, di_t[s], dz_t[s], 0, D2)
 
         def h_interleave(s):
-            hi_t[s] = mid.tile([P, D1, 4], BF16, name="hi", align_bytes=256)
-            interleave(nc.scalar.copy, hi_t[s], h_t[s])
+            hi_t[s] = mid.tile([P, D1, 4], BF16, name="hi", align_bytes=256, bufs=3)
+            cut = D1 if s < 5 else H_SPLIT
+            interleave(nc.scalar.copy, hi_t[s], h_t[s], 0, cut)
+            if cut < D1:
+                interleave(nc.vector.tensor_copy, hi_t[s], h_t[s], cut, D1)
 
         def product(s):
-            p_t[s] = mid.tile([P, 4, 4, P], F32, name="p")
+            p_t[s] = mid.tile([P, 4, 4, P], F32, name="p", bufs=3)
             pieces = [slice(j, j + 1) for j in range(4)] if s == 0 else [slice(0, 4)]
             for js in pieces:
                 nc.vector.tensor_tensor(
@@ -136,7 +138,7 @@ def tile_bnn_pb_v_kernel(tc, h0, wm1, wv1, bm1, bv1, we1, be1, z, grad_out, out_
             )
             if s == S - 1:
                 r = outs.tile([P, D2], F32, name="r%d" % b, bufs=1)
-                copy = nc.vector.tensor_copy if b < 2 else nc.scalar.copy
+                copy = nc.vector.tensor_copy if b % 2 == 0 else nc.scalar.copy
                 copy(out=r[:], in_=acc[b][:])
                 nc.sync.dma_start(out=out_1[P * b : P * (b + 1), :], in_=r[:])
 
@@ -156,11 +158,9 @@ def tile_bnn_pb_v_kernel(tc, h0, wm1, wv1, bm1, bv1, we1, be1, z, grad_out, out_
                 start=True,
                 stop=True,
             )
-            on_vector = (s == S - 1 and j % 2 == 1) or (s == S - 2 and j == 3)
-            copy = nc.vector.tensor_copy if on_vector else nc.scalar.copy
-            copy(out=o_t[s][:, j, :, :], in_=bank[:].rearrange("p t x -> p x t"))
-            if s == S - 1 and j % 2 == 1:
-                store_rows(s, j - 1, j + 1)
+            nc.scalar.copy(out=o_t[s][:, j, :, :], in_=bank[:].rearrange("p t x -> p x t"))
+            if s == S - 1:
+                store_rows(s, j, j + 1)
 
         def store_rows(s, j0, j1):
             nc.sync.dma_start(
@@ -176,30 +176,32 @@ def tile_bnn_pb_v_kernel(tc, h0, wm1, wv1, bm1, bv1, we1, be1, z, grad_out, out_
             return lambda s: fn(s, k)
 
         STEP = [
-            (sub(weight_grad, 2), 1),
-            (sub(w_transposes, 1), 0),
-            (sub(input_grad, 0), 1),
-            (sub(weight_grad, 1), 1),
-            (product, -2),
-            (sub(weight_grad, 3), 1),
-            (sub(w_transposes, 2), 0),
-            (q_d, -1),
-            (load, -3),
-            (sub(w_transposes, 3), 0),
+            (q_t, 0),
+            (load_zg, -3),
+            (load_h, -3),
+            (product, -3),
             (q_w, 0),
-            (sub(input_grad, 1), 1),
-            (sub(weight_grad, 0), 1),
-            (store, 2),
-            (mask, -2),
-            (sub(input_grad, 2), 1),
+            (h_interleave, -1),
+            (sub(w_transposes, 1), -1),
+            (sub(w_transposes, 2), -1),
+            (q_d, 1),
+            (sub(weight_grad, 0), 2),
+            (sub(weight_grad, 3), 2),
+            (q_h, 1),
+            (load_we, -5),
             (sub(dz_transposes, 0), -1),
+            (d_interleave, -1),
+            (store, 1),
             (sub(dz_transposes, 1), -1),
-            (q_t, -1),
-            (sub(w_transposes, 0), -1),
-            (h_interleave, -2),
-            (d_interleave, -2),
-            (q_h, -1),
-            (sub(input_grad, 3), 1),
+            (sub(weight_grad, 2), 2),
+            (sub(input_grad, 0), 0),
+            (sub(weight_grad, 1), 2),
+            (sub(input_grad, 1), 0),
+            (sub(input_grad, 2), 0),
+            (sub(w_transposes, 0), -2),
+            (mask, -2),
+            (sub(w_transposes, 3), -1),
+            (sub(input_grad, 3), 0),
         ]
 
         with tc.manual_schedule():
@@ -213,11 +215,9 @@ def tile_bnn_pb_v_kernel(tc, h0, wm1, wv1, bm1, bv1, we1, be1, z, grad_out, out_
             for js in (slice(0, 2), slice(2, 4)):
                 nc.sync.dma_start(out=wv_t[:, js, :], in_=wv_view[:, js, :])
                 nc.sync.dma_start(out=we_t[0][:, js, :], in_=we_view[:, js, :])
-            load_zg(0)
             wm_t = const.tile([P, 4, D2], BF16, name="wm_t")
             nc.sync.dma_start(out=wm_t[:], in_=wm1.rearrange("(p j) w -> p j w", j=4))
-            load_h(0)
-            load(1)
+            load_we(1)
 
             e_s = const.tile([P, 4, 4, P], F32, name="e_s")
             wm_s = const.tile([P, 4, 4, P], F32, name="wm_s")
@@ -238,8 +238,8 @@ def tile_bnn_pb_v_kernel(tc, h0, wm1, wv1, bm1, bv1, we1, be1, z, grad_out, out_
                     op1=ALU.add,
                 )
 
-            for step in range(-3, S + 3):
+            for step in range(-5, S + 2):
                 for what, lag in STEP:
                     s = step - lag
-                    if 0 <= s < S and not (what is load and s < 2):
+                    if 0 <= s < S and not (what is load_we and s < 2):
                         what(s)

@@ -17,7 +17,7 @@ ALU = mybir.AluOpType
 ACT = mybir.ActivationFunctionType
 
 P = 128
-H_SPLIT = 128
+H_SPLIT = 192
 
 
 def tile_bnn_pb_v_kernel(tc, h0, wm1, wv1, bm1, bv1, we1, be1, z, grad_out, out_0, out_1):
@@ -46,9 +46,13 @@ def tile_bnn_pb_v_kernel(tc, h0, wm1, wv1, bm1, bv1, we1, be1, z, grad_out, out_
 
         def load_zg(s):
             z_t[s] = loads.tile([P, 4, D2], F32, name="z")
-            nc.sync.dma_start(out=z_t[s][:], in_=z[s].rearrange("(p j) w -> p j w", j=4))
             g_t[s] = loads.tile([P, 4, D2], BF16, name="g")
-            nc.sync.dma_start(out=g_t[s][:], in_=grad_out[s].rearrange("(p j) w -> p j w", j=4))
+            for js in row_pieces(s):
+                nc.sync.dma_start(out=z_t[s][:, js, :], in_=z[s].rearrange("(p j) w -> p j w", j=4)[:, js, :])
+                nc.sync.dma_start(out=g_t[s][:, js, :], in_=grad_out[s].rearrange("(p j) w -> p j w", j=4)[:, js, :])
+
+        def row_pieces(s):
+            return [slice(0, 2), slice(2, 4)] if s == 0 else [slice(0, 4)]
 
         def load_h(s):
             h_t[s] = loads.tile([P, 4, D1], BF16, name="h")
@@ -74,7 +78,10 @@ def tile_bnn_pb_v_kernel(tc, h0, wm1, wv1, bm1, bv1, we1, be1, z, grad_out, out_
 
         def mask(s):
             dz_t[s] = mid.tile([P, 4, D2], BF16, name="dz", align_bytes=256, bufs=3)
-            nc.vector.scalar_tensor_tensor(out=dz_t[s][:], in0=z_t[s][:], scalar=0.0, in1=g_t[s][:], op0=ALU.is_gt, op1=ALU.mult)
+            for js in row_pieces(s):
+                nc.vector.scalar_tensor_tensor(
+                    out=dz_t[s][:, js, :], in0=z_t[s][:, js, :], scalar=0.0, in1=g_t[s][:, js, :], op0=ALU.is_gt, op1=ALU.mult
+                )
 
         def interleave(copy, out, in_, lo, hi):
             copy(
@@ -138,7 +145,7 @@ def tile_bnn_pb_v_kernel(tc, h0, wm1, wv1, bm1, bv1, we1, be1, z, grad_out, out_
             )
             if s == S - 1:
                 r = outs.tile([P, D2], F32, name="r%d" % b, bufs=1)
-                copy = nc.vector.tensor_copy if b % 2 == 0 else nc.scalar.copy
+                copy = nc.vector.tensor_copy if b in (1, 2) else nc.scalar.copy
                 copy(out=r[:], in_=acc[b][:])
                 nc.sync.dma_start(out=out_1[P * b : P * (b + 1), :], in_=r[:])
 
@@ -158,7 +165,8 @@ def tile_bnn_pb_v_kernel(tc, h0, wm1, wv1, bm1, bv1, we1, be1, z, grad_out, out_
                 start=True,
                 stop=True,
             )
-            nc.scalar.copy(out=o_t[s][:, j, :, :], in_=bank[:].rearrange("p t x -> p x t"))
+            copy = nc.vector.tensor_copy if s == S - 2 and j == 2 else nc.scalar.copy
+            copy(out=o_t[s][:, j, :, :], in_=bank[:].rearrange("p t x -> p x t"))
             if s == S - 1:
                 store_rows(s, j, j + 1)
 
@@ -176,32 +184,32 @@ def tile_bnn_pb_v_kernel(tc, h0, wm1, wv1, bm1, bv1, we1, be1, z, grad_out, out_
             return lambda s: fn(s, k)
 
         STEP = [
-            (q_t, 0),
-            (load_zg, -3),
-            (load_h, -3),
-            (product, -3),
-            (q_w, 0),
-            (h_interleave, -1),
-            (sub(w_transposes, 1), -1),
-            (sub(w_transposes, 2), -1),
-            (q_d, 1),
-            (sub(weight_grad, 0), 2),
-            (sub(weight_grad, 3), 2),
-            (q_h, 1),
-            (load_we, -5),
-            (sub(dz_transposes, 0), -1),
-            (d_interleave, -1),
-            (store, 1),
-            (sub(dz_transposes, 1), -1),
-            (sub(weight_grad, 2), 2),
             (sub(input_grad, 0), 0),
-            (sub(weight_grad, 1), 2),
             (sub(input_grad, 1), 0),
+            (sub(dz_transposes, 0), -1),
+            (sub(dz_transposes, 1), -1),
             (sub(input_grad, 2), 0),
-            (sub(w_transposes, 0), -2),
-            (mask, -2),
-            (sub(w_transposes, 3), -1),
             (sub(input_grad, 3), 0),
+            (product, -4),
+            (q_w, -1),
+            (sub(weight_grad, 1), 1),
+            (mask, -2),
+            (q_t, -1),
+            (load_we, -6),
+            (h_interleave, -2),
+            (sub(w_transposes, 0), -2),
+            (q_d, 0),
+            (q_h, 0),
+            (load_h, -4),
+            (sub(w_transposes, 1), -2),
+            (load_zg, -4),
+            (sub(weight_grad, 0), 1),
+            (sub(weight_grad, 3), 1),
+            (sub(w_transposes, 2), -2),
+            (sub(w_transposes, 3), -2),
+            (store, 0),
+            (sub(weight_grad, 2), 1),
+            (d_interleave, -2),
         ]
 
         with tc.manual_schedule():
@@ -217,7 +225,6 @@ def tile_bnn_pb_v_kernel(tc, h0, wm1, wv1, bm1, bv1, we1, be1, z, grad_out, out_
                 nc.sync.dma_start(out=we_t[0][:, js, :], in_=we_view[:, js, :])
             wm_t = const.tile([P, 4, D2], BF16, name="wm_t")
             nc.sync.dma_start(out=wm_t[:], in_=wm1.rearrange("(p j) w -> p j w", j=4))
-            load_we(1)
 
             e_s = const.tile([P, 4, 4, P], F32, name="e_s")
             wm_s = const.tile([P, 4, 4, P], F32, name="wm_s")
@@ -238,8 +245,8 @@ def tile_bnn_pb_v_kernel(tc, h0, wm1, wv1, bm1, bv1, we1, be1, z, grad_out, out_
                     op1=ALU.add,
                 )
 
-            for step in range(-5, S + 2):
+            for step in range(-6, S + 1):
                 for what, lag in STEP:
                     s = step - lag
-                    if 0 <= s < S and not (what is load_we and s < 2):
+                    if 0 <= s < S and not (what is load_we and s == 0):
                         what(s)

from contextlib import ExitStack

import concourse.mybir as mybir
from concourse.masks import make_identity

S, B, D1, D2 = 8, 512, 512, 512
FLOPS = 2 * 2 * S * B * D1 * D2
BYTES = S * B * (2 * D1 + 4 * D2 + 2 * D2 + 4 * D1) + 2 * S * D1 * D2 + (2 + 2 + 4) * D1 * D2

F32 = mybir.dt.float32
BF16 = mybir.dt.bfloat16
U32 = mybir.dt.uint32
U8 = mybir.dt.uint8
E4M3 = mybir.dt.float8_e4m3fn_x4
E5M2 = mybir.dt.float8_e5m2_x4
ALU = mybir.AluOpType
ACT = mybir.ActivationFunctionType

P = 128
H_SPLIT = 192


def tile_bnn_pb_v_kernel(tc, h0, wm1, wv1, bm1, bv1, we1, be1, z, grad_out, out_0, out_1):
    nc = tc.nc
    with ExitStack() as ctx:
        const = ctx.enter_context(tc.tile_pool(name="const", bufs=1))
        loads = ctx.enter_context(tc.tile_pool(name="loads", bufs=4))
        mid = ctx.enter_context(tc.tile_pool(name="mid", bufs=2))
        codes = ctx.enter_context(tc.tile_pool(name="codes", bufs=2))
        outs = ctx.enter_context(tc.tile_pool(name="outs", bufs=3))
        acc_pool = ctx.enter_context(tc.psum_pool(name="acc", bufs=1))
        psum = ctx.enter_context(tc.psum_pool(name="psum", bufs=4))

        ident_f = const.tile([P, P], F32, name="ident_f")
        make_identity(nc, ident_f[:])

        acc = [acc_pool.tile([P, D2], F32, name="acc%d" % b) for b in range(4)]

        we_t, z_t, g_t, h_t = {}, {}, {}, {}
        hi_t, di_t, p_t, wt_t, dz_t, dt_t = {}, {}, {}, {}, {}, {}
        wq_t, dq_t, hq_t, tq_t, o_t = {}, {}, {}, {}, {}

        def load_we(s):
            we_t[s] = loads.tile([P, 4, D2], BF16, name="we")
            nc.sync.dma_start(out=we_t[s][:], in_=we1[s].rearrange("(p j) w -> p j w", j=4))

        def load_zg(s):
            z_t[s] = loads.tile([P, 4, D2], F32, name="z")
            g_t[s] = loads.tile([P, 4, D2], BF16, name="g")
            for js in row_pieces(s):
                nc.sync.dma_start(out=z_t[s][:, js, :], in_=z[s].rearrange("(p j) w -> p j w", j=4)[:, js, :])
                nc.sync.dma_start(out=g_t[s][:, js, :], in_=grad_out[s].rearrange("(p j) w -> p j w", j=4)[:, js, :])

        def row_pieces(s):
            return [slice(0, 2), slice(2, 4)] if s == 0 else [slice(0, 4)]

        def load_h(s):
            h_t[s] = loads.tile([P, 4, D1], BF16, name="h")
            nc.sync.dma_start(out=h_t[s][:], in_=h0[s].rearrange("(p j) w -> p j w", j=4))

        def quantize(s, src, dtype, store, nm):
            c = codes.tile([P, 512], U32, name=nm + "c", align_bytes=256)
            q = codes.tile([P, 512], U8, name=nm + "s", align_bytes=256)
            nc.vector.quantize_mx(out=c[:].bitcast(dtype), scales=q[:], in_=src)
            store[s] = (c, q)

        def q_h(s):
            quantize(s, hi_t[s][:].rearrange("p w j -> p (w j)"), E4M3, hq_t, "h")

        def q_d(s):
            quantize(s, di_t[s][:].rearrange("p w j -> p (w j)"), E5M2, dq_t, "d")

        def q_w(s):
            quantize(s, wt_t[s][:].rearrange("p j x t -> p (j x t)"), E4M3, wq_t, "w")

        def q_t(s):
            quantize(s, dt_t[s][:].rearrange("p j x u -> p (j x u)").bitcast(BF16), E5M2, tq_t, "t")

        def mask(s):
            dz_t[s] = mid.tile([P, 4, D2], BF16, name="dz", align_bytes=256, bufs=3)
            for js in row_pieces(s):
                nc.vector.scalar_tensor_tensor(
                    out=dz_t[s][:, js, :], in0=z_t[s][:, js, :], scalar=0.0, in1=g_t[s][:, js, :], op0=ALU.is_gt, op1=ALU.mult
                )

        def interleave(copy, out, in_, lo, hi):
            copy(
                out=out[:, lo:hi, :].rearrange("p (c i) t -> p c t i", i=4),
                in_=in_[:, :, lo:hi].rearrange("p t (c i) -> p c t i", i=4),
            )

        def d_interleave(s):
            di_t[s] = mid.tile([P, D2, 4], BF16, name="di", align_bytes=256)
            interleave(nc.vector.tensor_copy, di_t[s], dz_t[s], 0, D2)

        def h_interleave(s):
            hi_t[s] = mid.tile([P, D1, 4], BF16, name="hi", align_bytes=256, bufs=3)
            cut = D1 if s < 5 else H_SPLIT
            interleave(nc.scalar.copy, hi_t[s], h_t[s], 0, cut)
            if cut < D1:
                interleave(nc.vector.tensor_copy, hi_t[s], h_t[s], cut, D1)

        def product(s):
            p_t[s] = mid.tile([P, 4, 4, P], F32, name="p", bufs=3)
            pieces = [slice(j, j + 1) for j in range(4)] if s == 0 else [slice(0, 4)]
            for js in pieces:
                nc.vector.tensor_tensor(
                    out=p_t[s][:, js, :, :],
                    in0=we_t[s][:, js, :].rearrange("p j (m t) -> p j t m", t=4),
                    in1=e_s[:, js, :, :],
                    op=ALU.mult,
                )

        def w_transposes(s, j):
            if j == 0:
                wt_t[s] = mid.tile([P, 4, P, 4], BF16, name="wt", align_bytes=256)
            bank = psum.tile([P, 4, P], F32, name="bank")
            for t in range(4):
                nc.tensor.matmul(bank[:, t, :], lhsT=wm_s[:, j, t, :], rhs=ident_f[:], is_transpose=True, start=True, stop=False)
                nc.tensor.matmul(bank[:, t, :], lhsT=p_t[s][:, j, t, :], rhs=ident_f[:], is_transpose=True, start=False, stop=True)
            nc.scalar.copy(out=wt_t[s][:, j, :, :], in_=bank[:].rearrange("p t x -> p x t"))

        def dz_transposes(s, half):
            if half == 0:
                dt_t[s] = mid.tile([P, 4, P, 2], F32, name="dt", align_bytes=256)
            bank = psum.tile([P, 2, 2, P], F32, name="bank")
            for k in range(2):
                words = dz_t[s][:, 2 * half + k, :].bitcast(F32)
                for u in range(2):
                    nc.tensor.transpose(bank[:, k, u, :], words[:, u::2], ident_f[:])
            nc.scalar.copy(out=dt_t[s][:, 2 * half : 2 * half + 2, :, :], in_=bank[:].rearrange("p k u x -> p k x u"))

        def weight_grad(s, b):
            hc, hs = hq_t[s]
            dc, ds = dq_t[s]
            cols = slice(P * b, P * (b + 1))
            nc.tensor.matmul_mx(
                out=acc[b][:],
                lhsT=hc[:, cols].bitcast(E4M3),
                lhsT_scale=hs[:, cols],
                rhs=dc[:].bitcast(E5M2),
                rhs_scale=ds[:],
                start=(s == 0),
                stop=(s == S - 1),
            )
            if s == S - 1:
                r = outs.tile([P, D2], F32, name="r%d" % b, bufs=1)
                copy = nc.vector.tensor_copy if b in (1, 2) else nc.scalar.copy
                copy(out=r[:], in_=acc[b][:])
                nc.sync.dma_start(out=out_1[P * b : P * (b + 1), :], in_=r[:])

        def input_grad(s, j):
            tcod, tsc = tq_t[s]
            wc, ws = wq_t[s]
            if j == 0:
                o_t[s] = outs.tile([P, 4, P, 4], F32, name="o")
            cols = slice(P * j, P * (j + 1))
            bank = psum.tile([P, 4, P], F32, name="bank")
            nc.tensor.matmul_mx(
                out=bank[:].rearrange("p t x -> p (t x)"),
                lhsT=tcod[:, cols].bitcast(E5M2),
                lhsT_scale=tsc[:, cols],
                rhs=wc[:].bitcast(E4M3),
                rhs_scale=ws[:],
                start=True,
                stop=True,
            )
            copy = nc.vector.tensor_copy if s == S - 2 and j == 2 else nc.scalar.copy
            copy(out=o_t[s][:, j, :, :], in_=bank[:].rearrange("p t x -> p x t"))
            if s == S - 1:
                store_rows(s, j, j + 1)

        def store_rows(s, j0, j1):
            nc.sync.dma_start(
                out=out_0[s].rearrange("(p j) d -> p j d", j=4)[:, j0:j1, :],
                in_=o_t[s][:, j0:j1, :, :].rearrange("p j x t -> p j (x t)"),
            )

        def store(s):
            if s < S - 1:
                store_rows(s, 0, 4)

        def sub(fn, k):
            return lambda s: fn(s, k)

        STEP = [
            (sub(input_grad, 0), 0),
            (sub(input_grad, 1), 0),
            (sub(dz_transposes, 0), -1),
            (sub(dz_transposes, 1), -1),
            (sub(input_grad, 2), 0),
            (sub(input_grad, 3), 0),
            (product, -4),
            (q_w, -1),
            (sub(weight_grad, 1), 1),
            (mask, -2),
            (q_t, -1),
            (load_we, -6),
            (h_interleave, -2),
            (sub(w_transposes, 0), -2),
            (q_d, 0),
            (q_h, 0),
            (load_h, -4),
            (sub(w_transposes, 1), -2),
            (load_zg, -4),
            (sub(weight_grad, 0), 1),
            (sub(weight_grad, 3), 1),
            (sub(w_transposes, 2), -2),
            (sub(w_transposes, 3), -2),
            (store, 0),
            (sub(weight_grad, 2), 1),
            (d_interleave, -2),
        ]

        with tc.manual_schedule():
            warm = const.tile([P, 1], F32, name="warm")
            nc.vector.memset(warm[:], 0.0)
            nc.scalar.activation(out=warm[:], in_=warm[:], func=ACT.Exp)
            wv_t = const.tile([P, 4, D2], BF16, name="wv_t")
            wv_view = wv1.rearrange("(p j) w -> p j w", j=4)
            we_t[0] = loads.tile([P, 4, D2], BF16, name="we")
            we_view = we1[0].rearrange("(p j) w -> p j w", j=4)
            for js in (slice(0, 2), slice(2, 4)):
                nc.sync.dma_start(out=wv_t[:, js, :], in_=wv_view[:, js, :])
                nc.sync.dma_start(out=we_t[0][:, js, :], in_=we_view[:, js, :])
            wm_t = const.tile([P, 4, D2], BF16, name="wm_t")
            nc.sync.dma_start(out=wm_t[:], in_=wm1.rearrange("(p j) w -> p j w", j=4))

            e_s = const.tile([P, 4, 4, P], F32, name="e_s")
            wm_s = const.tile([P, 4, 4, P], F32, name="wm_s")
            for j in range(4):
                nc.scalar.activation(
                    out=e_s[:, j, :, :],
                    in_=wv_t[:, j, :].rearrange("p (m t) -> p t m", t=4),
                    func=ACT.Exp,
                    scale=0.5,
                )
            for j in range(4):
                nc.gpsimd.tensor_scalar(
                    out=wm_s[:, j, :, :],
                    in0=wm_t[:, j, :].rearrange("p (m t) -> p t m", t=4),
                    scalar1=1.0,
                    scalar2=0.0,
                    op0=ALU.mult,
                    op1=ALU.add,
                )

            for step in range(-6, S + 1):
                for what, lag in STEP:
                    s = step - lag
                    if 0 <= s < S and not (what is load_we and s == 0):
                        what(s)
